import numpy as np
import ml_dtypes


def mxq(x, axis, fmt="e4m3"):
    dtype, down = {"e4m3": (ml_dtypes.float8_e4m3fn, 7), "e5m2": (ml_dtypes.float8_e5m2, 14)}[fmt]
    v = np.moveaxis(np.asarray(x, np.float32).astype(ml_dtypes.bfloat16).astype(np.float64), axis, -1)
    blocks = v.reshape(v.shape[:-1] + (-1, 32))
    amax = np.abs(blocks).max(-1, keepdims=True)
    byte = np.maximum(np.where(amax > 0, np.frexp(amax)[1] - 1 + 127, 0) - down, 1)
    scale = np.exp2(byte - 127.0)
    codes = (blocks / scale).astype(np.float32).astype(dtype).astype(np.float64)
    return np.moveaxis((codes * scale).reshape(v.shape), -1, axis)


WIDE = False


def mx_kscale(k):
    if not WIDE:
        return np.ones(k)
    levels = np.array([10, -10, 5, -5, 0])
    if k % 512:
        return np.exp2(np.random.permutation(np.resize(levels, k // 32))).repeat(32)
    a = np.empty((k // 512, 16))
    for p in range(k // 512):
        a[p, :8] = np.random.permutation(np.resize(levels, 8))
        for g in range(8):
            far = levels[np.abs(levels - a[p, g]) >= 10]
            a[p, g + 8] = far[np.random.randint(len(far))]
    return np.exp2(a.ravel()).repeat(32)


BF16 = ml_dtypes.bfloat16


def bf(x):
    return np.asarray(x, np.float32).astype(BF16)


def f64(x):
    return np.asarray(x).astype(np.float64)


M, P, D = 2048, 2048, 512


def setup_inputs():
    s = mx_kscale(P)
    return {"G": bf(np.exp(-np.abs(3.0 + np.random.standard_normal((M, P)))) * s[None, :]),
            "x_next": bf(np.random.standard_normal((P, D)) * 1.5 * (s.mean() / s)[:, None])}


def reference(G, x_next):
    g = f64(G)
    p = g / np.sum(g, axis=1, keepdims=True)
    return mxq(p, 1, "e4m3") @ mxq(f64(x_next), 0, "e4m3")

@@ -1,0 +1,189 @@
+from contextlib import ExitStack
+
+import concourse.mybir as mybir
+from concourse.masks import make_identity
+
+BF16 = mybir.dt.bfloat16
+F32 = mybir.dt.float32
+U32 = mybir.dt.uint32
+U8 = mybir.dt.uint8
+FP8X4 = mybir.dt.float8_e4m3fn_x4
+ALU = mybir.AluOpType
+
+P = 128
+M, K, D = 2048, 2048, 512
+NT = M // P
+NG = K // 512
+FLOPS = 2 * M * K * D
+
+
+def tile_nntransformlearner_pb_kernel(tc, G, x_next, out):
+    nc = tc.nc
+    with ExitStack() as ctx:
+        const = ctx.enter_context(tc.tile_pool(name="const", bufs=1))
+        gpool = ctx.enter_context(tc.tile_pool(name="gpool", bufs=NT))
+        xpool = ctx.enter_context(tc.tile_pool(name="xpool", bufs=NG))
+        work = ctx.enter_context(tc.tile_pool(name="work", bufs=4))
+        stat = ctx.enter_context(tc.tile_pool(name="stat", bufs=NT))
+        opool = ctx.enter_context(tc.tile_pool(name="opool", bufs=6))
+        tpsum = ctx.enter_context(tc.psum_pool(name="tpsum", bufs=6))
+        apsum = ctx.enter_context(tc.psum_pool(name="apsum", bufs=2))
+        ctx.enter_context(tc.manual_schedule())
+
+        ident = const.tile([P, P], F32, name="ident")
+        make_identity(nc, ident[:])
+        x_codes = const.tile([P, NG, D], U32, name="x_codes", align_bytes=64)
+        x_scales = const.tile([P, NG, D], U8, name="x_scales", align_bytes=64)
+
+        g_tiles = {}
+        x_raw = {}
+        x_grp = {}
+        rsums = {}
+        rinvs = {}
+        p_tiles = {}
+        xt_tiles = {}
+        grp_tiles = {}
+        code_tiles = {}
+        acc_tiles = {}
+
+        def load_g(i):
+            g_sb = gpool.tile([P, K], BF16, name="g_sb")
+            nc.sync.dma_start(out=g_sb[:], in_=G[i * P:(i + 1) * P, :])
+            g_tiles[i] = g_sb
+
+        def load_x(g):
+            x_sb = xpool.tile([P, 2, 2 * D], BF16, name="x_sb")
+            rows = x_next[g * 512:(g + 1) * 512, :].rearrange("(h u j e) d -> j h u (e d)", u=2, j=2, e=2)
+            for j in range(2):
+                nc.sync.dma_start(out=x_sb[j:P:2, :, :], in_=rows[j])
+            x_raw[g] = x_sb
+
+        def rs(i):
+            junk = work.tile([P, K], BF16, name="junk", bufs=2)
+            rsum = stat.tile([P, 1], F32, name="rsum")
+            nc.vector.tensor_scalar(
+                out=junk[:], in0=g_tiles[i][:], scalar1=1.0, scalar2=None,
+                op0=ALU.mult, op1=ALU.add, accum_out=rsum[:],
+            )
+            rsums[i] = rsum
+
+        def rc(i):
+            rinv = stat.tile([P, 1], F32, name="rinv")
+            nc.vector.reciprocal(out=rinv[:], in_=rsums[i][:])
+            rinvs[i] = rinv
+
+        def sc(i):
+            p_sb = work.tile([P, 2, K // 2], BF16, name="p_sb")
+            nc.vector.tensor_scalar(
+                out=p_sb[:].rearrange("p u (h f) -> p u h f", f=4),
+                in0=g_tiles[i][:].rearrange("p (h u f) -> p u h f", u=2, f=4),
+                scalar1=rinvs[i][:, 0:1], scalar2=None, op0=ALU.mult,
+            )
+            p_tiles[i] = p_sb
+
+        def tr(i):
+            words = p_tiles[i][:].bitcast(F32)
+            for h in range(2):
+                xt = tpsum.tile([P, 2, 2, P], F32, name="xt")
+                for gg in range(2):
+                    for u in range(2):
+                        w0 = (2 * h + gg) * P
+                        nc.tensor.transpose(xt[:, gg, u, :], words[:, u, w0:w0 + P], ident[:])
+                xt_tiles[(i, h)] = xt
+
+        def cp(i, h, eng="S"):
+            if h == 0:
+                grouped = work.tile([P, NG, P, 4], BF16, name="grouped", align_bytes=64)
+                grp_tiles[i] = grouped
+            dst = grp_tiles[i][:].bitcast(F32)[:, 2 * h:2 * h + 2, :, :]
+            src = xt_tiles[(i, h)][:].rearrange("p g u m -> p g m u")
+            if eng == "S":
+                nc.scalar.copy(out=dst, in_=src)
+            else:
+                nc.vector.tensor_copy(out=dst, in_=src)
+
+        def xr(g, eng="S"):
+            xg = xpool.tile([P, D, 4], BF16, name="xg", align_bytes=64)
+            dst = xg[:].rearrange("p (c i) t -> p c t i", i=4)
+            src = x_raw[g][:].rearrange("p u (e c i) -> p c (u e) i", e=2, i=4)
+            if eng == "S":
+                nc.scalar.copy(out=dst, in_=src)
+            else:
+                nc.vector.tensor_copy(out=dst, in_=src)
+            x_grp[g] = xg
+
+        def xq(g):
+            nc.vector.quantize_mx(
+                out=x_codes[:, g, :].bitcast(FP8X4),
+                scales=x_scales[:, g, :],
+                in_=x_grp[g][:].rearrange("p d t -> p (d t)"),
+            )
+
+        def qz(i, g0=0, g1=NG):
+            if g0 == 0:
+                codes = work.tile([P, NG * P], U32, name="codes", align_bytes=64)
+                scales = work.tile([P, NG * P], U8, name="scales", align_bytes=64)
+                code_tiles[i] = (codes, scales)
+            codes, scales = code_tiles[i]
+            nc.vector.quantize_mx(
+                out=codes[:, g0 * P:g1 * P].bitcast(FP8X4),
+                scales=scales[:, g0 * P:g1 * P],
+                in_=grp_tiles[i][:, g0:g1, :, :].rearrange("p g m t -> p (g m t)"),
+            )
+
+        def mm(i, g0=0, g1=NG):
+            codes, scales = code_tiles[i]
+            if g0 == 0:
+                acc = apsum.tile([P, D], F32, name="acc")
+                acc_tiles[i] = acc
+            acc = acc_tiles[i]
+            for g in range(g0, g1):
+                nc.tensor.matmul_mx(
+                    out=acc[:],
+                    lhsT=codes[:, g * P:(g + 1) * P].bitcast(FP8X4),
+                    lhsT_scale=scales[:, g * P:(g + 1) * P],
+                    rhs=x_codes[:, g, :].bitcast(FP8X4),
+                    rhs_scale=x_scales[:, g, :],
+                    start=(g == 0),
+                    stop=(g == NG - 1),
+                )
+
+        def ot(i, eng="S"):
+            o_sb = opool.tile([P, D], F32, name="o_sb")
+            if eng == "S":
+                nc.scalar.copy(out=o_sb[:], in_=acc_tiles[i][:])
+            else:
+                nc.vector.tensor_copy(out=o_sb[:], in_=acc_tiles[i][:])
+            nc.sync.dma_start(out=out[i * P:(i + 1) * P, :], in_=o_sb[:])
+
+        for i in range(4):
+            load_g(i)
+            load_x(i)
+        for i in range(4, NT):
+            load_g(i)
+
+        xr(0)
+        rs(0); rc(0); sc(0); tr(0)
+        cp(0, 0); cp(0, 1); xr(1)
+        rs(1); rc(1); sc(1); tr(1)
+        cp(1, 0); xr(2); cp(1, 1)
+        rs(2); xq(0); rc(2); sc(2); tr(2)
+        xr(3); cp(2, 0); cp(2, 1)
+        rs(3); xq(1); rc(3); qz(0); sc(3); tr(3)
+        cp(3, 0); cp(3, 1)
+        rs(4); xq(2); rc(4); xq(3); qz(1)
+        mm(0); mm(1); ot(0); ot(1)
+        for j in range(4, NT):
+            if j + 1 < NT:
+                rs(j + 1)
+            sc(j); tr(j)
+            if j + 1 < NT:
+                rc(j + 1)
+            cp(j, 0)
+            qz(j - 2); mm(j - 2)
+            ot(j - 2)
+            cp(j, 1)
+        qz(14); mm(14); ot(14)
+        qz(15, 0, 2); mm(15, 0, 2)
+        qz(15, 2, 4); mm(15, 2, 4)
+        ot(15, "V")

@@ -35,6 +35,11 @@ def tile_nntransformlearner_pb_kernel(tc, G, x_next, out):
         x_codes = const.tile([P, NG, D], U32, name="x_codes", align_bytes=64)
         x_scales = const.tile([P, NG, D], U8, name="x_scales", align_bytes=64)
 
+        warm = const.tile([P, 1], F32, name="warm")
+        warm_out = const.tile([P, 1], F32, name="warm_out")
+        nc.gpsimd.memset(warm[:], 0.0)
+        nc.scalar.copy(out=warm_out[:], in_=warm[:])
+
         g_tiles = {}
         x_raw = {}
         x_grp = {}
@@ -148,13 +153,13 @@ def tile_nntransformlearner_pb_kernel(tc, G, x_next, out):
                     stop=(g == NG - 1),
                 )
 
-        def ot(i, eng="S"):
-            o_sb = opool.tile([P, D], F32, name="o_sb")
+        def ot(i, eng="S", d0=0, d1=D):
+            o_sb = opool.tile([P, d1 - d0], F32, name="o_sb")
             if eng == "S":
-                nc.scalar.copy(out=o_sb[:], in_=acc_tiles[i][:])
+                nc.scalar.copy(out=o_sb[:], in_=acc_tiles[i][:, d0:d1])
             else:
-                nc.vector.tensor_copy(out=o_sb[:], in_=acc_tiles[i][:])
-            nc.sync.dma_start(out=out[i * P:(i + 1) * P, :], in_=o_sb[:])
+                nc.vector.tensor_copy(out=o_sb[:], in_=acc_tiles[i][:, d0:d1])
+            nc.sync.dma_start(out=out[i * P:(i + 1) * P, d0:d1], in_=o_sb[:])
 
         for i in range(4):
             load_g(i)
@@ -173,17 +178,20 @@ def tile_nntransformlearner_pb_kernel(tc, G, x_next, out):
         cp(3, 0); cp(3, 1)
         rs(4); xq(2); rc(4); xq(3); qz(1)
         mm(0); mm(1); ot(0); ot(1)
-        for j in range(4, NT):
-            if j + 1 < NT:
-                rs(j + 1)
+        qz(2); mm(2); ot(2)
+        for j in range(4, NT - 1):
+            rs(j + 1)
             sc(j); tr(j)
-            if j + 1 < NT:
-                rc(j + 1)
-            cp(j, 0)
-            qz(j - 2); mm(j - 2)
-            ot(j - 2)
-            cp(j, 1)
-        qz(14); mm(14); ot(14)
-        qz(15, 0, 2); mm(15, 0, 2)
-        qz(15, 2, 4); mm(15, 2, 4)
-        ot(15, "V")
+            rc(j + 1)
+            cp(j, 0); cp(j, 1)
+            qz(j - 1); mm(j - 1)
+            ot(j - 1)
+        last = NT - 1
+        sc(last); tr(last)
+        cp(last, 0)
+        qz(last - 1); mm(last - 1)
+        cp(last, 1, "V")
+        qz(last, 0, 2); mm(last, 0, 2)
+        qz(last, 2, 4); mm(last, 2, 4)
+        ot(last - 1)
+        ot(last, "V", 0, D // 2); ot(last, "S", D // 2, D)

@@ -9,12 +9,16 @@ U32 = mybir.dt.uint32
 U8 = mybir.dt.uint8
 FP8X4 = mybir.dt.float8_e4m3fn_x4
 ALU = mybir.AluOpType
+ACT = mybir.ActivationFunctionType
 
 P = 128
 M, K, D = 2048, 2048, 512
 NT = M // P
 NG = K // 512
 FLOPS = 2 * M * K * D
+SPLIT_FROM = 4
+S_COLS = 352
+AHEAD = 3
 
 
 def tile_nntransformlearner_pb_kernel(tc, G, x_next, out):
@@ -43,6 +47,7 @@ def tile_nntransformlearner_pb_kernel(tc, G, x_next, out):
         g_tiles = {}
         x_raw = {}
         x_grp = {}
+        parts = {}
         rsums = {}
         rinvs = {}
         p_tiles = {}
@@ -63,11 +68,21 @@ def tile_nntransformlearner_pb_kernel(tc, G, x_next, out):
                 nc.sync.dma_start(out=x_sb[j:P:2, :, :], in_=rows[j])
             x_raw[g] = x_sb
 
+        def part(i):
+            junk_s = work.tile([P, S_COLS], BF16, name="junk_s", bufs=2)
+            psum_s = stat.tile([P, 1], F32, name="psum_s")
+            nc.scalar.activation(
+                out=junk_s[:], in_=g_tiles[i][:, 0:S_COLS], func=ACT.Copy, accum_out=psum_s[:],
+            )
+            parts[i] = psum_s
+
         def rs(i):
-            junk = work.tile([P, K], BF16, name="junk", bufs=2)
+            c0 = S_COLS if i in parts else 0
+            junk = work.tile([P, K - c0], BF16, name="junk", bufs=2)
             rsum = stat.tile([P, 1], F32, name="rsum")
             nc.vector.tensor_scalar(
-                out=junk[:], in0=g_tiles[i][:], scalar1=1.0, scalar2=None,
+                out=junk[:], in0=g_tiles[i][:, c0:K], scalar1=1.0,
+                scalar2=parts[i][:, 0:1] if i in parts else None,
                 op0=ALU.mult, op1=ALU.add, accum_out=rsum[:],
             )
             rsums[i] = rsum
@@ -161,36 +176,41 @@ def tile_nntransformlearner_pb_kernel(tc, G, x_next, out):
                 nc.vector.tensor_copy(out=o_sb[:], in_=acc_tiles[i][:, d0:d1])
             nc.sync.dma_start(out=out[i * P:(i + 1) * P, d0:d1], in_=o_sb[:])
 
-        for i in range(4):
-            load_g(i)
-            load_x(i)
-        for i in range(4, NT):
+        load_g(0); load_x(0); load_x(1); load_g(1); load_x(2); load_g(2); load_x(3)
+        for i in range(3, NT):
             load_g(i)
 
         xr(0)
         rs(0); rc(0); sc(0); tr(0)
-        cp(0, 0); cp(0, 1); xr(1)
-        rs(1); rc(1); sc(1); tr(1)
-        cp(1, 0); xr(2); cp(1, 1)
-        rs(2); xq(0); rc(2); sc(2); tr(2)
-        xr(3); cp(2, 0); cp(2, 1)
-        rs(3); xq(1); rc(3); qz(0); sc(3); tr(3)
-        cp(3, 0); cp(3, 1)
-        rs(4); xq(2); rc(4); xq(3); qz(1)
-        mm(0); mm(1); ot(0); ot(1)
-        qz(2); mm(2); ot(2)
-        for j in range(4, NT - 1):
-            rs(j + 1)
+        xr(1, "V"); cp(0, 0); cp(0, 1)
+        xq(0); xq(1)
+        xr(2)
+        rs(1); qz(0); rc(1); sc(1); tr(1)
+        xr(3); xq(2)
+        rs(2); cp(1, 0); cp(1, 1); rc(2)
+        part(4)
+        rs(3); sc(2); tr(2)
+        xq(3); rc(3); qz(1)
+        cp(2, 0); cp(2, 1)
+        part(5)
+        mm(0); mm(1); ot(0)
+        for j in range(3, NT):
+            if j + 1 < NT:
+                rs(j + 1)
             sc(j); tr(j)
-            rc(j + 1)
-            cp(j, 0); cp(j, 1)
+            if j + 1 < NT:
+                rc(j + 1)
+            cp(j, 0)
+            if j < NT - 1:
+                cp(j, 1)
             qz(j - 1); mm(j - 1)
-            ot(j - 1)
+            if j + AHEAD < NT:
+                part(j + AHEAD)
+            if j < NT - 1:
+                ot(j - 2)
         last = NT - 1
-        sc(last); tr(last)
-        cp(last, 0)
-        qz(last - 1); mm(last - 1)
         cp(last, 1, "V")
+        ot(last - 2)
         qz(last, 0, 2); mm(last, 0, 2)
         qz(last, 2, 4); mm(last, 2, 4)
         ot(last - 1)

@@ -16,9 +16,8 @@ M, K, D = 2048, 2048, 512
 NT = M // P
 NG = K // 512
 FLOPS = 2 * M * K * D
-SPLIT_FROM = 4
 S_COLS = 352
-AHEAD = 3
+AHEAD = 4
 
 
 def tile_nntransformlearner_pb_kernel(tc, G, x_next, out):
@@ -151,19 +150,17 @@ def tile_nntransformlearner_pb_kernel(tc, G, x_next, out):
                 in_=grp_tiles[i][:, g0:g1, :, :].rearrange("p g m t -> p (g m t)"),
             )
 
-        def mm(i, g0=0, g1=NG):
+        def mm(i, d0=0, d1=D):
             codes, scales = code_tiles[i]
-            if g0 == 0:
-                acc = apsum.tile([P, D], F32, name="acc")
-                acc_tiles[i] = acc
-            acc = acc_tiles[i]
-            for g in range(g0, g1):
+            acc = apsum.tile([P, d1 - d0], F32, name="acc")
+            acc_tiles[(i, d0)] = acc
+            for g in range(NG):
                 nc.tensor.matmul_mx(
                     out=acc[:],
                     lhsT=codes[:, g * P:(g + 1) * P].bitcast(FP8X4),
                     lhsT_scale=scales[:, g * P:(g + 1) * P],
-                    rhs=x_codes[:, g, :].bitcast(FP8X4),
-                    rhs_scale=x_scales[:, g, :],
+                    rhs=x_codes[:, g, d0:d1].bitcast(FP8X4),
+                    rhs_scale=x_scales[:, g, d0:d1],
                     start=(g == 0),
                     stop=(g == NG - 1),
                 )
@@ -171,9 +168,9 @@ def tile_nntransformlearner_pb_kernel(tc, G, x_next, out):
         def ot(i, eng="S", d0=0, d1=D):
             o_sb = opool.tile([P, d1 - d0], F32, name="o_sb")
             if eng == "S":
-                nc.scalar.copy(out=o_sb[:], in_=acc_tiles[i][:, d0:d1])
+                nc.scalar.copy(out=o_sb[:], in_=acc_tiles[(i, d0)][:])
             else:
-                nc.vector.tensor_copy(out=o_sb[:], in_=acc_tiles[i][:, d0:d1])
+                nc.vector.tensor_copy(out=o_sb[:], in_=acc_tiles[(i, d0)][:])
             nc.sync.dma_start(out=out[i * P:(i + 1) * P, d0:d1], in_=o_sb[:])
 
         load_g(0); load_x(0); load_x(1); load_g(1); load_x(2); load_g(2); load_x(3)
@@ -183,35 +180,37 @@ def tile_nntransformlearner_pb_kernel(tc, G, x_next, out):
         xr(0)
         rs(0); rc(0); sc(0); tr(0)
         xr(1, "V"); cp(0, 0); cp(0, 1)
-        xq(0); xq(1)
+        xq(0); rs(1); xq(1); rc(1)
         xr(2)
-        rs(1); qz(0); rc(1); sc(1); tr(1)
-        xr(3); xq(2)
-        rs(2); cp(1, 0); cp(1, 1); rc(2)
+        sc(1); tr(1)
+        qz(0); rs(2)
+        xr(3)
+        xq(2); rc(2); sc(2); tr(2)
+        cp(1, 0); cp(1, 1)
         part(4)
-        rs(3); sc(2); tr(2)
-        xq(3); rc(3); qz(1)
+        rs(3); xq(3); rc(3)
         cp(2, 0); cp(2, 1)
         part(5)
-        mm(0); mm(1); ot(0)
+        qz(1); rs(4)
+        mm(0); mm(1)
+        part(6)
+        ot(0)
+        last = NT - 1
         for j in range(3, NT):
-            if j + 1 < NT:
-                rs(j + 1)
             sc(j); tr(j)
             if j + 1 < NT:
                 rc(j + 1)
+            if j + 2 < NT:
+                rs(j + 2)
             cp(j, 0)
-            if j < NT - 1:
+            if j < last:
                 cp(j, 1)
             qz(j - 1); mm(j - 1)
             if j + AHEAD < NT:
                 part(j + AHEAD)
-            if j < NT - 1:
-                ot(j - 2)
-        last = NT - 1
+            ot(j - 2)
         cp(last, 1, "V")
-        ot(last - 2)
-        qz(last, 0, 2); mm(last, 0, 2)
-        qz(last, 2, 4); mm(last, 2, 4)
-        ot(last - 1)
+        qz(last, 0, 2); qz(last, 2, 4)
+        ot(last - 1, "V")
+        mm(last, 0, D // 2); mm(last, D // 2, D)
         ot(last, "V", 0, D // 2); ot(last, "S", D // 2, D)

@@ -16,8 +16,12 @@ M, K, D = 2048, 2048, 512
 NT = M // P
 NG = K // 512
 FLOPS = 2 * M * K * D
-S_COLS = 352
-AHEAD = 4
+FOLD_AHEAD = 5
+SUM_AHEAD = 4
+
+
+def on_tensor(i):
+    return i < NT and i in (2, 5, 8, 11)
 
 
 def tile_nntransformlearner_pb_kernel(tc, G, x_next, out):
@@ -29,12 +33,15 @@ def tile_nntransformlearner_pb_kernel(tc, G, x_next, out):
         work = ctx.enter_context(tc.tile_pool(name="work", bufs=4))
         stat = ctx.enter_context(tc.tile_pool(name="stat", bufs=NT))
         opool = ctx.enter_context(tc.tile_pool(name="opool", bufs=6))
-        tpsum = ctx.enter_context(tc.psum_pool(name="tpsum", bufs=6))
-        apsum = ctx.enter_context(tc.psum_pool(name="apsum", bufs=2))
+        tpsum = ctx.enter_context(tc.psum_pool(name="tpsum", bufs=4))
+        apsum = ctx.enter_context(tc.psum_pool(name="apsum", bufs=3))
+        spsum = ctx.enter_context(tc.psum_pool(name="spsum", bufs=1))
         ctx.enter_context(tc.manual_schedule())
 
         ident = const.tile([P, P], F32, name="ident")
         make_identity(nc, ident[:])
+        ident_bf = const.tile([P, P], BF16, name="ident_bf")
+        nc.gpsimd.tensor_copy(out=ident_bf[:], in_=ident[:])
         x_codes = const.tile([P, NG, D], U32, name="x_codes", align_bytes=64)
         x_scales = const.tile([P, NG, D], U8, name="x_scales", align_bytes=64)
 
@@ -46,7 +53,7 @@ def tile_nntransformlearner_pb_kernel(tc, G, x_next, out):
         g_tiles = {}
         x_raw = {}
         x_grp = {}
-        parts = {}
+        fold_tiles = {}
         rsums = {}
         rinvs = {}
         p_tiles = {}
@@ -67,23 +74,34 @@ def tile_nntransformlearner_pb_kernel(tc, G, x_next, out):
                 nc.sync.dma_start(out=x_sb[j:P:2, :, :], in_=rows[j])
             x_raw[g] = x_sb
 
-        def part(i):
-            junk_s = work.tile([P, S_COLS], BF16, name="junk_s", bufs=2)
-            psum_s = stat.tile([P, 1], F32, name="psum_s")
-            nc.scalar.activation(
-                out=junk_s[:], in_=g_tiles[i][:, 0:S_COLS], func=ACT.Copy, accum_out=psum_s[:],
-            )
-            parts[i] = psum_s
-
         def rs(i):
-            c0 = S_COLS if i in parts else 0
-            junk = work.tile([P, K - c0], BF16, name="junk", bufs=2)
+            if on_tensor(i):
+                return
+            junk = work.tile([P, K], BF16, name="junk", bufs=2)
             rsum = stat.tile([P, 1], F32, name="rsum")
             nc.vector.tensor_scalar(
-                out=junk[:], in0=g_tiles[i][:, c0:K], scalar1=1.0,
-                scalar2=parts[i][:, 0:1] if i in parts else None,
+                out=junk[:], in0=g_tiles[i][:], scalar1=1.0, scalar2=None,
                 op0=ALU.mult, op1=ALU.add, accum_out=rsum[:],
             )
+            rsums[i] = rsum
+
+        def fold(i):
+            if not on_tensor(i):
+                return
+            folded = spsum.tile([P, 512], F32, name="folded")
+            for c in range(4):
+                nc.tensor.matmul(
+                    out=folded[:], lhsT=ident_bf[:], rhs=g_tiles[i][:, c * 512:(c + 1) * 512],
+                    start=(c == 0), stop=(c == 3),
+                )
+            fold_tiles[i] = folded
+
+        def fs(i):
+            if not on_tensor(i):
+                return
+            junk_s = work.tile([P, 512], BF16, name="junk_s", bufs=2)
+            rsum = stat.tile([P, 1], F32, name="rsum")
+            nc.scalar.activation(out=junk_s[:], in_=fold_tiles[i][:], func=ACT.Copy, accum_out=rsum[:])
             rsums[i] = rsum
 
         def rc(i):
@@ -180,22 +198,23 @@ def tile_nntransformlearner_pb_kernel(tc, G, x_next, out):
         xr(0)
         rs(0); rc(0); sc(0); tr(0)
         xr(1, "V"); cp(0, 0); cp(0, 1)
-        xq(0); rs(1); xq(1); rc(1)
+        xq(0); rs(1); xq(1); fold(2); rc(1)
         xr(2)
         sc(1); tr(1)
-        qz(0); rs(2)
+        qz(0); fs(2)
         xr(3)
         xq(2); rc(2); sc(2); tr(2)
         cp(1, 0); cp(1, 1)
-        part(4)
         rs(3); xq(3); rc(3)
+        fold(5)
         cp(2, 0); cp(2, 1)
-        part(5)
         qz(1); rs(4)
         mm(0); mm(1)
-        part(6)
+        fs(5); fs(6)
         ot(0)
         last = NT - 1
+        quantised = 2
+        emptied = 1
         for j in range(3, NT):
             sc(j); tr(j)
             if j + 1 < NT:
@@ -205,12 +224,19 @@ def tile_nntransformlearner_pb_kernel(tc, G, x_next, out):
             cp(j, 0)
             if j < last:
                 cp(j, 1)
-            qz(j - 1); mm(j - 1)
-            if j + AHEAD < NT:
-                part(j + AHEAD)
-            ot(j - 2)
+            fs(j + SUM_AHEAD)
+            ready = quantised
+            lag = 2 if j < last - 1 else 1
+            for i in range(quantised, j - lag + 1):
+                qz(i); mm(i)
+            quantised = j - lag + 1
+            fold(j + FOLD_AHEAD)
+            for i in range(emptied, ready):
+                ot(i)
+            emptied = ready
         cp(last, 1, "V")
         qz(last, 0, 2); qz(last, 2, 4)
-        ot(last - 1, "V")
+        for i in range(emptied, last):
+            ot(i, "S" if i < last - 1 else "V")
         mm(last, 0, D // 2); mm(last, D // 2, D)
         ot(last, "V", 0, D // 2); ot(last, "S", D // 2, D)

@@ -16,12 +16,11 @@ M, K, D = 2048, 2048, 512
 NT = M // P
 NG = K // 512
 FLOPS = 2 * M * K * D
-FOLD_AHEAD = 5
-SUM_AHEAD = 4
+SUM_AHEAD = 3
 
 
-def on_tensor(i):
-    return i < NT and i in (2, 5, 8, 11)
+def on_scalar(i):
+    return i > 0 and i % 5 == 0
 
 
 def tile_nntransformlearner_pb_kernel(tc, G, x_next, out):
@@ -33,27 +32,25 @@ def tile_nntransformlearner_pb_kernel(tc, G, x_next, out):
         work = ctx.enter_context(tc.tile_pool(name="work", bufs=4))
         stat = ctx.enter_context(tc.tile_pool(name="stat", bufs=NT))
         opool = ctx.enter_context(tc.tile_pool(name="opool", bufs=6))
-        tpsum = ctx.enter_context(tc.psum_pool(name="tpsum", bufs=4))
+        tpsum = ctx.enter_context(tc.psum_pool(name="tpsum", bufs=5))
         apsum = ctx.enter_context(tc.psum_pool(name="apsum", bufs=3))
-        spsum = ctx.enter_context(tc.psum_pool(name="spsum", bufs=1))
         ctx.enter_context(tc.manual_schedule())
 
         ident = const.tile([P, P], F32, name="ident")
         make_identity(nc, ident[:])
-        ident_bf = const.tile([P, P], BF16, name="ident_bf")
-        nc.gpsimd.tensor_copy(out=ident_bf[:], in_=ident[:])
         x_codes = const.tile([P, NG, D], U32, name="x_codes", align_bytes=64)
         x_scales = const.tile([P, NG, D], U8, name="x_scales", align_bytes=64)
 
         warm = const.tile([P, 1], F32, name="warm")
         warm_out = const.tile([P, 1], F32, name="warm_out")
         nc.gpsimd.memset(warm[:], 0.0)
+        minus_one = const.tile([P, 1], F32, name="minus_one")
+        nc.gpsimd.memset(minus_one[:], -1.0)
         nc.scalar.copy(out=warm_out[:], in_=warm[:])
 
         g_tiles = {}
         x_raw = {}
         x_grp = {}
-        fold_tiles = {}
         rsums = {}
         rinvs = {}
         p_tiles = {}
@@ -74,39 +71,25 @@ def tile_nntransformlearner_pb_kernel(tc, G, x_next, out):
                 nc.sync.dma_start(out=x_sb[j:P:2, :, :], in_=rows[j])
             x_raw[g] = x_sb
 
-        def rs(i):
-            if on_tensor(i):
-                return
-            junk = work.tile([P, K], BF16, name="junk", bufs=2)
+        def rs(i, eng="V"):
             rsum = stat.tile([P, 1], F32, name="rsum")
-            nc.vector.tensor_scalar(
-                out=junk[:], in0=g_tiles[i][:], scalar1=1.0, scalar2=None,
-                op0=ALU.mult, op1=ALU.add, accum_out=rsum[:],
-            )
-            rsums[i] = rsum
-
-        def fold(i):
-            if not on_tensor(i):
-                return
-            folded = spsum.tile([P, 512], F32, name="folded")
-            for c in range(4):
-                nc.tensor.matmul(
-                    out=folded[:], lhsT=ident_bf[:], rhs=g_tiles[i][:, c * 512:(c + 1) * 512],
-                    start=(c == 0), stop=(c == 3),
+            if eng == "V":
+                junk = work.tile([P, K], BF16, name="junk", bufs=2)
+                nc.vector.tensor_scalar(
+                    out=junk[:], in0=g_tiles[i][:], scalar1=1.0, scalar2=None,
+                    op0=ALU.mult, op1=ALU.add, accum_out=rsum[:],
                 )
-            fold_tiles[i] = folded
-
-        def fs(i):
-            if not on_tensor(i):
-                return
-            junk_s = work.tile([P, 512], BF16, name="junk_s", bufs=2)
-            rsum = stat.tile([P, 1], F32, name="rsum")
-            nc.scalar.activation(out=junk_s[:], in_=fold_tiles[i][:], func=ACT.Copy, accum_out=rsum[:])
+            else:
+                junk_s = work.tile([P, K], BF16, name="junk_s", bufs=2)
+                nc.scalar.activation(out=junk_s[:], in_=g_tiles[i][:], func=ACT.Copy, accum_out=rsum[:])
             rsums[i] = rsum
 
-        def rc(i):
+        def rc(i, eng="G"):
             rinv = stat.tile([P, 1], F32, name="rinv")
-            nc.vector.reciprocal(out=rinv[:], in_=rsums[i][:])
+            if eng == "G":
+                nc.gpsimd.tensor_tensor(out=rinv[:], in0=rsums[i][:], in1=minus_one[:], op=ALU.pow)
+            else:
+                nc.vector.reciprocal(out=rinv[:], in_=rsums[i][:])
             rinvs[i] = rinv
 
         def sc(i):
@@ -196,47 +179,43 @@ def tile_nntransformlearner_pb_kernel(tc, G, x_next, out):
             load_g(i)
 
         xr(0)
-        rs(0); rc(0); sc(0); tr(0)
-        xr(1, "V"); cp(0, 0); cp(0, 1)
-        xq(0); rs(1); xq(1); fold(2); rc(1)
-        xr(2)
+        rs(0); rc(0, "V"); sc(0); tr(0)
+        cp(0, 0); cp(0, 1)
+        xr(1, "V"); rs(1); rc(1)
+        xr(2); xr(3)
+        xq(1); rs(2); rc(2); xq(0)
         sc(1); tr(1)
-        qz(0); fs(2)
-        xr(3)
-        xq(2); rc(2); sc(2); tr(2)
-        cp(1, 0); cp(1, 1)
-        rs(3); xq(3); rc(3)
-        fold(5)
-        cp(2, 0); cp(2, 1)
-        qz(1); rs(4)
+        qz(0)
+        sc(2); tr(2)
+        xq(2); xq(3)
+        cp(1, 0); cp(1, 1); cp(2, 0); cp(2, 1)
+        rs(3); rc(3)
+        qz(1)
         mm(0); mm(1)
-        fs(5); fs(6)
-        ot(0)
+        rs(5, "S")
         last = NT - 1
         quantised = 2
-        emptied = 1
+        emptied = 0
         for j in range(3, NT):
+            if j < last and not on_scalar(j + 1):
+                rs(j + 1)
             sc(j); tr(j)
-            if j + 1 < NT:
+            if j < last:
                 rc(j + 1)
-            if j + 2 < NT:
-                rs(j + 2)
             cp(j, 0)
             if j < last:
                 cp(j, 1)
-            fs(j + SUM_AHEAD)
-            ready = quantised
-            lag = 2 if j < last - 1 else 1
+            if j + SUM_AHEAD < NT and on_scalar(j + SUM_AHEAD):
+                rs(j + SUM_AHEAD, "S")
+            lag = 2 if j < last else 1
             for i in range(quantised, j - lag + 1):
                 qz(i); mm(i)
             quantised = j - lag + 1
-            fold(j + FOLD_AHEAD)
-            for i in range(emptied, ready):
+            for i in range(emptied, j - 1):
                 ot(i)
-            emptied = ready
+            emptied = j - 1
         cp(last, 1, "V")
         qz(last, 0, 2); qz(last, 2, 4)
-        for i in range(emptied, last):
-            ot(i, "S" if i < last - 1 else "V")
+        ot(last - 1, "V")
         mm(last, 0, D // 2); mm(last, D // 2, D)
         ot(last, "V", 0, D // 2); ot(last, "S", D // 2, D)

@@ -16,11 +16,11 @@ M, K, D = 2048, 2048, 512
 NT = M // P
 NG = K // 512
 FLOPS = 2 * M * K * D
-SUM_AHEAD = 3
+SUM_AHEAD = 4
 
 
 def on_scalar(i):
-    return i > 0 and i % 5 == 0
+    return i in (5, 9, 13)
 
 
 def tile_nntransformlearner_pb_kernel(tc, G, x_next, out):
@@ -44,8 +44,6 @@ def tile_nntransformlearner_pb_kernel(tc, G, x_next, out):
         warm = const.tile([P, 1], F32, name="warm")
         warm_out = const.tile([P, 1], F32, name="warm_out")
         nc.gpsimd.memset(warm[:], 0.0)
-        minus_one = const.tile([P, 1], F32, name="minus_one")
-        nc.gpsimd.memset(minus_one[:], -1.0)
         nc.scalar.copy(out=warm_out[:], in_=warm[:])
 
         g_tiles = {}
@@ -84,12 +82,9 @@ def tile_nntransformlearner_pb_kernel(tc, G, x_next, out):
                 nc.scalar.activation(out=junk_s[:], in_=g_tiles[i][:], func=ACT.Copy, accum_out=rsum[:])
             rsums[i] = rsum
 
-        def rc(i, eng="G"):
+        def rc(i):
             rinv = stat.tile([P, 1], F32, name="rinv")
-            if eng == "G":
-                nc.gpsimd.tensor_tensor(out=rinv[:], in0=rsums[i][:], in1=minus_one[:], op=ALU.pow)
-            else:
-                nc.vector.reciprocal(out=rinv[:], in_=rsums[i][:])
+            nc.vector.reciprocal(out=rinv[:], in_=rsums[i][:])
             rinvs[i] = rinv
 
         def sc(i):
@@ -179,33 +174,34 @@ def tile_nntransformlearner_pb_kernel(tc, G, x_next, out):
             load_g(i)
 
         xr(0)
-        rs(0); rc(0, "V"); sc(0); tr(0)
+        rs(0); rc(0); sc(0); tr(0)
         cp(0, 0); cp(0, 1)
-        xr(1, "V"); rs(1); rc(1)
+        xr(1, "V"); rs(1)
         xr(2); xr(3)
-        xq(1); rs(2); rc(2); xq(0)
+        xq(1); rc(1); rs(2); xq(0); rc(2)
         sc(1); tr(1)
         qz(0)
         sc(2); tr(2)
         xq(2); xq(3)
         cp(1, 0); cp(1, 1); cp(2, 0); cp(2, 1)
-        rs(3); rc(3)
+        rs(3)
         qz(1)
+        rc(3); rs(4)
         mm(0); mm(1)
         rs(5, "S")
         last = NT - 1
         quantised = 2
         emptied = 0
         for j in range(3, NT):
-            if j < last and not on_scalar(j + 1):
-                rs(j + 1)
             sc(j); tr(j)
             if j < last:
                 rc(j + 1)
+            if j + 2 < NT and not on_scalar(j + 2):
+                rs(j + 2)
             cp(j, 0)
             if j < last:
                 cp(j, 1)
-            if j + SUM_AHEAD < NT and on_scalar(j + SUM_AHEAD):
+            if on_scalar(j + SUM_AHEAD):
                 rs(j + SUM_AHEAD, "S")
             lag = 2 if j < last else 1
             for i in range(quantised, j - lag + 1):

@@ -20,7 +20,7 @@ SUM_AHEAD = 4
 
 
 def on_scalar(i):
-    return i in (5, 9, 13)
+    return i in (1, 4, 6, 10, 14)
 
 
 def tile_nntransformlearner_pb_kernel(tc, G, x_next, out):
@@ -169,26 +169,25 @@ def tile_nntransformlearner_pb_kernel(tc, G, x_next, out):
                 nc.vector.tensor_copy(out=o_sb[:], in_=acc_tiles[(i, d0)][:])
             nc.sync.dma_start(out=out[i * P:(i + 1) * P, d0:d1], in_=o_sb[:])
 
-        load_g(0); load_x(0); load_x(1); load_g(1); load_x(2); load_g(2); load_x(3)
+        load_g(0); load_g(1); load_g(2); load_x(0); load_x(2); load_x(1); load_x(3)
         for i in range(3, NT):
             load_g(i)
 
-        xr(0)
+        rs(1, "S")
         rs(0); rc(0); sc(0); tr(0)
-        cp(0, 0); cp(0, 1)
-        xr(1, "V"); rs(1)
-        xr(2); xr(3)
-        xq(1); rc(1); rs(2); xq(0); rc(2)
-        sc(1); tr(1)
+        xr(0); xr(1)
+        rs(2); rc(1); sc(1); tr(1)
+        rc(2); xr(2, "V"); sc(2); tr(2)
+        xr(3, "V")
+        cp(0, 0); cp(0, 1); cp(1, 0); cp(1, 1)
+        xq(0); rs(3); xq(1)
         qz(0)
-        sc(2); tr(2)
-        xq(2); xq(3)
-        cp(1, 0); cp(1, 1); cp(2, 0); cp(2, 1)
-        rs(3)
+        rs(4, "S")
+        cp(2, 0); cp(2, 1)
+        xq(2); xq(3); rc(3)
         qz(1)
-        rc(3); rs(4)
         mm(0); mm(1)
-        rs(5, "S")
+        rs(6, "S")
         last = NT - 1
         quantised = 2
         emptied = 0
@@ -201,17 +200,18 @@ def tile_nntransformlearner_pb_kernel(tc, G, x_next, out):
             cp(j, 0)
             if j < last:
                 cp(j, 1)
-            if on_scalar(j + SUM_AHEAD):
+            if j + SUM_AHEAD > 6 and on_scalar(j + SUM_AHEAD):
                 rs(j + SUM_AHEAD, "S")
+            for i in range(emptied, j - 2):
+                ot(i)
+            emptied = j - 2
             lag = 2 if j < last else 1
             for i in range(quantised, j - lag + 1):
                 qz(i); mm(i)
             quantised = j - lag + 1
-            for i in range(emptied, j - 1):
-                ot(i)
-            emptied = j - 1
         cp(last, 1, "V")
         qz(last, 0, 2); qz(last, 2, 4)
+        ot(last - 2)
         ot(last - 1, "V")
         mm(last, 0, D // 2); mm(last, D // 2, D)
         ot(last, "V", 0, D // 2); ot(last, "S", D // 2, D)

@@ -20,7 +20,7 @@ SUM_AHEAD = 4
 
 
 def on_scalar(i):
-    return i in (1, 4, 6, 10, 14)
+    return i in (1, 6, 9, 13)
 
 
 def tile_nntransformlearner_pb_kernel(tc, G, x_next, out):
@@ -38,6 +38,8 @@ def tile_nntransformlearner_pb_kernel(tc, G, x_next, out):
 
         ident = const.tile([P, P], F32, name="ident")
         make_identity(nc, ident[:])
+        ident_bf = const.tile([P, P], BF16, name="ident_bf")
+        nc.gpsimd.tensor_copy(out=ident_bf[:], in_=ident[:])
         x_codes = const.tile([P, NG, D], U32, name="x_codes", align_bytes=64)
         x_scales = const.tile([P, NG, D], U8, name="x_scales", align_bytes=64)
 
@@ -49,6 +51,7 @@ def tile_nntransformlearner_pb_kernel(tc, G, x_next, out):
         g_tiles = {}
         x_raw = {}
         x_grp = {}
+        fold_tiles = {}
         rsums = {}
         rinvs = {}
         p_tiles = {}
@@ -80,6 +83,21 @@ def tile_nntransformlearner_pb_kernel(tc, G, x_next, out):
             else:
                 junk_s = work.tile([P, K], BF16, name="junk_s", bufs=2)
                 nc.scalar.activation(out=junk_s[:], in_=g_tiles[i][:], func=ACT.Copy, accum_out=rsum[:])
+            rsums[i] = rsum
+
+        def fold(i):
+            folded = apsum.tile([P, 512], F32, name="acc")
+            for c in range(4):
+                nc.tensor.matmul(
+                    out=folded[:], lhsT=ident_bf[:], rhs=g_tiles[i][:, c * 512:(c + 1) * 512],
+                    start=(c == 0), stop=(c == 3),
+                )
+            fold_tiles[i] = folded
+
+        def fs(i):
+            junk_f = work.tile([P, 512], BF16, name="junk_f", bufs=1)
+            rsum = stat.tile([P, 1], F32, name="rsum")
+            nc.scalar.activation(out=junk_f[:], in_=fold_tiles[i][:], func=ACT.Copy, accum_out=rsum[:])
             rsums[i] = rsum
 
         def rc(i):
@@ -182,8 +200,9 @@ def tile_nntransformlearner_pb_kernel(tc, G, x_next, out):
         cp(0, 0); cp(0, 1); cp(1, 0); cp(1, 1)
         xq(0); rs(3); xq(1)
         qz(0)
-        rs(4, "S")
+        fold(4)
         cp(2, 0); cp(2, 1)
+        fs(4)
         xq(2); xq(3); rc(3)
         qz(1)
         mm(0); mm(1)

@@ -60,9 +60,11 @@ def tile_nntransformlearner_pb_kernel(tc, G, x_next, out):
         code_tiles = {}
         acc_tiles = {}
 
-        def load_g(i):
+        def load_g(i, pieces=1):
             g_sb = gpool.tile([P, K], BF16, name="g_sb")
-            nc.sync.dma_start(out=g_sb[:], in_=G[i * P:(i + 1) * P, :])
+            w = K // pieces
+            for c in range(pieces):
+                nc.sync.dma_start(out=g_sb[:, c * w:(c + 1) * w], in_=G[i * P:(i + 1) * P, c * w:(c + 1) * w])
             g_tiles[i] = g_sb
 
         def load_x(g):
@@ -84,6 +86,19 @@ def tile_nntransformlearner_pb_kernel(tc, G, x_next, out):
                 junk_s = work.tile([P, K], BF16, name="junk_s", bufs=2)
                 nc.scalar.activation(out=junk_s[:], in_=g_tiles[i][:], func=ACT.Copy, accum_out=rsum[:])
             rsums[i] = rsum
+
+        def rs_in_halves(i):
+            total = None
+            for c in range(2):
+                junk_h = work.tile([P, K // 2], BF16, name="junk_h", bufs=2)
+                rsum = stat.tile([P, 1], F32, name="rsum_h", bufs=2)
+                nc.vector.tensor_scalar(
+                    out=junk_h[:], in0=g_tiles[i][:, c * (K // 2):(c + 1) * (K // 2)], scalar1=1.0,
+                    scalar2=None if total is None else total[:, 0:1],
+                    op0=ALU.mult, op1=ALU.add, accum_out=rsum[:],
+                )
+                total = rsum
+            rsums[i] = total
 
         def fold(i):
             folded = apsum.tile([P, 512], F32, name="acc")
@@ -187,18 +202,18 @@ def tile_nntransformlearner_pb_kernel(tc, G, x_next, out):
                 nc.vector.tensor_copy(out=o_sb[:], in_=acc_tiles[(i, d0)][:])
             nc.sync.dma_start(out=out[i * P:(i + 1) * P, d0:d1], in_=o_sb[:])
 
-        load_g(0); load_g(1); load_g(2); load_x(0); load_x(2); load_x(1); load_x(3)
+        load_g(0, 2); load_g(1); load_g(2); load_x(0); load_x(2); load_x(1); load_x(3)
         for i in range(3, NT):
             load_g(i)
 
         rs(1, "S")
-        rs(0); rc(0); sc(0); tr(0)
+        rs_in_halves(0); rc(0); sc(0); tr(0)
         xr(0); xr(1)
         rs(2); rc(1); sc(1); tr(1)
         rc(2); xr(2, "V"); sc(2); tr(2)
-        xr(3, "V")
+        xq(0); xr(3, "V")
         cp(0, 0); cp(0, 1); cp(1, 0); cp(1, 1)
-        xq(0); rs(3); xq(1)
+        rs(3); xq(1)
         qz(0)
         fold(4)
         cp(2, 0); cp(2, 1)

from contextlib import ExitStack

import concourse.mybir as mybir
from concourse.masks import make_identity

BF16 = mybir.dt.bfloat16
F32 = mybir.dt.float32
U32 = mybir.dt.uint32
U8 = mybir.dt.uint8
FP8X4 = mybir.dt.float8_e4m3fn_x4
ALU = mybir.AluOpType
ACT = mybir.ActivationFunctionType

P = 128
M, K, D = 2048, 2048, 512
NT = M // P
NG = K // 512
FLOPS = 2 * M * K * D
SUM_AHEAD = 4


def on_scalar(i):
    return i in (1, 6, 9, 13)


def tile_nntransformlearner_pb_kernel(tc, G, x_next, out):
    nc = tc.nc
    with ExitStack() as ctx:
        const = ctx.enter_context(tc.tile_pool(name="const", bufs=1))
        gpool = ctx.enter_context(tc.tile_pool(name="gpool", bufs=NT))
        xpool = ctx.enter_context(tc.tile_pool(name="xpool", bufs=NG))
        work = ctx.enter_context(tc.tile_pool(name="work", bufs=4))
        stat = ctx.enter_context(tc.tile_pool(name="stat", bufs=NT))
        opool = ctx.enter_context(tc.tile_pool(name="opool", bufs=6))
        tpsum = ctx.enter_context(tc.psum_pool(name="tpsum", bufs=5))
        apsum = ctx.enter_context(tc.psum_pool(name="apsum", bufs=3))
        ctx.enter_context(tc.manual_schedule())

        ident = const.tile([P, P], F32, name="ident")
        make_identity(nc, ident[:])
        ident_bf = const.tile([P, P], BF16, name="ident_bf")
        nc.gpsimd.tensor_copy(out=ident_bf[:], in_=ident[:])
        x_codes = const.tile([P, NG, D], U32, name="x_codes", align_bytes=64)
        x_scales = const.tile([P, NG, D], U8, name="x_scales", align_bytes=64)

        warm = const.tile([P, 1], F32, name="warm")
        warm_out = const.tile([P, 1], F32, name="warm_out")
        nc.gpsimd.memset(warm[:], 0.0)
        nc.scalar.copy(out=warm_out[:], in_=warm[:])

        g_tiles = {}
        x_raw = {}
        x_grp = {}
        fold_tiles = {}
        rsums = {}
        rinvs = {}
        p_tiles = {}
        xt_tiles = {}
        grp_tiles = {}
        code_tiles = {}
        acc_tiles = {}

        def load_g(i, pieces=1):
            g_sb = gpool.tile([P, K], BF16, name="g_sb")
            w = K // pieces
            for c in range(pieces):
                nc.sync.dma_start(out=g_sb[:, c * w:(c + 1) * w], in_=G[i * P:(i + 1) * P, c * w:(c + 1) * w])
            g_tiles[i] = g_sb

        def load_x(g):
            x_sb = xpool.tile([P, 2, 2 * D], BF16, name="x_sb")
            rows = x_next[g * 512:(g + 1) * 512, :].rearrange("(h u j e) d -> j h u (e d)", u=2, j=2, e=2)
            for j in range(2):
                nc.sync.dma_start(out=x_sb[j:P:2, :, :], in_=rows[j])
            x_raw[g] = x_sb

        def rs(i, eng="V"):
            rsum = stat.tile([P, 1], F32, name="rsum")
            if eng == "V":
                junk = work.tile([P, K], BF16, name="junk", bufs=2)
                nc.vector.tensor_scalar(
                    out=junk[:], in0=g_tiles[i][:], scalar1=1.0, scalar2=None,
                    op0=ALU.mult, op1=ALU.add, accum_out=rsum[:],
                )
            else:
                junk_s = work.tile([P, K], BF16, name="junk_s", bufs=2)
                nc.scalar.activation(out=junk_s[:], in_=g_tiles[i][:], func=ACT.Copy, accum_out=rsum[:])
            rsums[i] = rsum

        def rs_in_halves(i):
            total = None
            for c in range(2):
                junk_h = work.tile([P, K // 2], BF16, name="junk_h", bufs=2)
                rsum = stat.tile([P, 1], F32, name="rsum_h", bufs=2)
                nc.vector.tensor_scalar(
                    out=junk_h[:], in0=g_tiles[i][:, c * (K // 2):(c + 1) * (K // 2)], scalar1=1.0,
                    scalar2=None if total is None else total[:, 0:1],
                    op0=ALU.mult, op1=ALU.add, accum_out=rsum[:],
                )
                total = rsum
            rsums[i] = total

        def fold(i):
            folded = apsum.tile([P, 512], F32, name="acc")
            for c in range(4):
                nc.tensor.matmul(
                    out=folded[:], lhsT=ident_bf[:], rhs=g_tiles[i][:, c * 512:(c + 1) * 512],
                    start=(c == 0), stop=(c == 3),
                )
            fold_tiles[i] = folded

        def fs(i):
            junk_f = work.tile([P, 512], BF16, name="junk_f", bufs=1)
            rsum = stat.tile([P, 1], F32, name="rsum")
            nc.scalar.activation(out=junk_f[:], in_=fold_tiles[i][:], func=ACT.Copy, accum_out=rsum[:])
            rsums[i] = rsum

        def rc(i):
            rinv = stat.tile([P, 1], F32, name="rinv")
            nc.vector.reciprocal(out=rinv[:], in_=rsums[i][:])
            rinvs[i] = rinv

        def sc(i):
            p_sb = work.tile([P, 2, K // 2], BF16, name="p_sb")
            nc.vector.tensor_scalar(
                out=p_sb[:].rearrange("p u (h f) -> p u h f", f=4),
                in0=g_tiles[i][:].rearrange("p (h u f) -> p u h f", u=2, f=4),
                scalar1=rinvs[i][:, 0:1], scalar2=None, op0=ALU.mult,
            )
            p_tiles[i] = p_sb

        def tr(i):
            words = p_tiles[i][:].bitcast(F32)
            for h in range(2):
                xt = tpsum.tile([P, 2, 2, P], F32, name="xt")
                for gg in range(2):
                    for u in range(2):
                        w0 = (2 * h + gg) * P
                        nc.tensor.transpose(xt[:, gg, u, :], words[:, u, w0:w0 + P], ident[:])
                xt_tiles[(i, h)] = xt

        def cp(i, h, eng="S"):
            if h == 0:
                grouped = work.tile([P, NG, P, 4], BF16, name="grouped", align_bytes=64)
                grp_tiles[i] = grouped
            dst = grp_tiles[i][:].bitcast(F32)[:, 2 * h:2 * h + 2, :, :]
            src = xt_tiles[(i, h)][:].rearrange("p g u m -> p g m u")
            if eng == "S":
                nc.scalar.copy(out=dst, in_=src)
            else:
                nc.vector.tensor_copy(out=dst, in_=src)

        def xr(g, eng="S"):
            xg = xpool.tile([P, D, 4], BF16, name="xg", align_bytes=64)
            dst = xg[:].rearrange("p (c i) t -> p c t i", i=4)
            src = x_raw[g][:].rearrange("p u (e c i) -> p c (u e) i", e=2, i=4)
            if eng == "S":
                nc.scalar.copy(out=dst, in_=src)
            else:
                nc.vector.tensor_copy(out=dst, in_=src)
            x_grp[g] = xg

        def xq(g):
            nc.vector.quantize_mx(
                out=x_codes[:, g, :].bitcast(FP8X4),
                scales=x_scales[:, g, :],
                in_=x_grp[g][:].rearrange("p d t -> p (d t)"),
            )

        def qz(i, g0=0, g1=NG):
            if g0 == 0:
                codes = work.tile([P, NG * P], U32, name="codes", align_bytes=64)
                scales = work.tile([P, NG * P], U8, name="scales", align_bytes=64)
                code_tiles[i] = (codes, scales)
            codes, scales = code_tiles[i]
            nc.vector.quantize_mx(
                out=codes[:, g0 * P:g1 * P].bitcast(FP8X4),
                scales=scales[:, g0 * P:g1 * P],
                in_=grp_tiles[i][:, g0:g1, :, :].rearrange("p g m t -> p (g m t)"),
            )

        def mm(i, d0=0, d1=D):
            codes, scales = code_tiles[i]
            acc = apsum.tile([P, d1 - d0], F32, name="acc")
            acc_tiles[(i, d0)] = acc
            for g in range(NG):
                nc.tensor.matmul_mx(
                    out=acc[:],
                    lhsT=codes[:, g * P:(g + 1) * P].bitcast(FP8X4),
                    lhsT_scale=scales[:, g * P:(g + 1) * P],
                    rhs=x_codes[:, g, d0:d1].bitcast(FP8X4),
                    rhs_scale=x_scales[:, g, d0:d1],
                    start=(g == 0),
                    stop=(g == NG - 1),
                )

        def ot(i, eng="S", d0=0, d1=D):
            o_sb = opool.tile([P, d1 - d0], F32, name="o_sb")
            if eng == "S":
                nc.scalar.copy(out=o_sb[:], in_=acc_tiles[(i, d0)][:])
            else:
                nc.vector.tensor_copy(out=o_sb[:], in_=acc_tiles[(i, d0)][:])
            nc.sync.dma_start(out=out[i * P:(i + 1) * P, d0:d1], in_=o_sb[:])

        load_g(0, 2); load_g(1); load_g(2); load_x(0); load_x(2); load_x(1); load_x(3)
        for i in range(3, NT):
            load_g(i)

        rs(1, "S")
        rs_in_halves(0); rc(0); sc(0); tr(0)
        xr(0); xr(1)
        rs(2); rc(1); sc(1); tr(1)
        rc(2); xr(2, "V"); sc(2); tr(2)
        xq(0); xr(3, "V")
        cp(0, 0); cp(0, 1); cp(1, 0); cp(1, 1)
        rs(3); xq(1)
        qz(0)
        fold(4)
        cp(2, 0); cp(2, 1)
        fs(4)
        xq(2); xq(3); rc(3)
        qz(1)
        mm(0); mm(1)
        rs(6, "S")
        last = NT - 1
        quantised = 2
        emptied = 0
        for j in range(3, NT):
            sc(j); tr(j)
            if j < last:
                rc(j + 1)
            if j + 2 < NT and not on_scalar(j + 2):
                rs(j + 2)
            cp(j, 0)
            if j < last:
                cp(j, 1)
            if j + SUM_AHEAD > 6 and on_scalar(j + SUM_AHEAD):
                rs(j + SUM_AHEAD, "S")
            for i in range(emptied, j - 2):
                ot(i)
            emptied = j - 2
            lag = 2 if j < last else 1
            for i in range(quantised, j - lag + 1):
                qz(i); mm(i)
            quantised = j - lag + 1
        cp(last, 1, "V")
        qz(last, 0, 2); qz(last, 2, 4)
        ot(last - 2)
        ot(last - 1, "V")
        mm(last, 0, D // 2); mm(last, D // 2, D)
        ot(last, "V", 0, D // 2); ot(last, "S", D // 2, D)
